import numpy as np
import ml_dtypes


def mxq(x, axis, fmt="e4m3"):
    dtype, down = {"e4m3": (ml_dtypes.float8_e4m3fn, 7), "e5m2": (ml_dtypes.float8_e5m2, 14)}[fmt]
    v = np.moveaxis(np.asarray(x, np.float32).astype(ml_dtypes.bfloat16).astype(np.float64), axis, -1)
    blocks = v.reshape(v.shape[:-1] + (-1, 32))
    amax = np.abs(blocks).max(-1, keepdims=True)
    byte = np.maximum(np.where(amax > 0, np.frexp(amax)[1] - 1 + 127, 0) - down, 1)
    scale = np.exp2(byte - 127.0)
    codes = (blocks / scale).astype(np.float32).astype(dtype).astype(np.float64)
    return np.moveaxis((codes * scale).reshape(v.shape), -1, axis)


WIDE = False


def mx_kscale(k):
    if not WIDE:
        return np.ones(k)
    levels = np.array([10, -10, 5, -5, 0])
    if k % 512:
        return np.exp2(np.random.permutation(np.resize(levels, k // 32))).repeat(32)
    a = np.empty((k // 512, 16))
    for p in range(k // 512):
        a[p, :8] = np.random.permutation(np.resize(levels, 8))
        for g in range(8):
            far = levels[np.abs(levels - a[p, g]) >= 10]
            a[p, g + 8] = far[np.random.randint(len(far))]
    return np.exp2(a.ravel()).repeat(32)


BF16 = ml_dtypes.bfloat16


def bf(x):
    return np.asarray(x, np.float32).astype(BF16)


def f64(x):
    return np.asarray(x).astype(np.float64)


B, HW, C, HID, WS, SS, HEADS = 1, 32, 1024, 2048, 8, 4, 16
L = HW * HW
NH = HW // WS
HD = C // HEADS
EPS = 1e-5


def ln(x, w, b):
    m = x.mean(-1, keepdims=True)
    xm = x - m
    v = np.mean(xm * xm, axis=-1, keepdims=True)
    return xm * (1.0 / np.sqrt(v + EPS)) * w + b


def setup_inputs():
    s = mx_kscale(C)
    return {"x": bf(np.random.standard_normal((B, L, C))),
            "ln1_w": bf((1.0 + 0.1 * np.random.standard_normal(C)) * s),
            "ln1_b": bf(0.1 * np.random.standard_normal(C) * s),
            "in_proj_w": bf(np.random.standard_normal((3 * C, C)) / np.sqrt(C) / s[None, :]),
            "in_proj_b": bf(0.1 * np.random.standard_normal(3 * C))}


def reference(x, ln1_w, ln1_b, in_proj_w, in_proj_b):
    h = ln(f64(x), f64(ln1_w), f64(ln1_b)).reshape(B, HW, HW, C)
    h = np.roll(h, (-SS, -SS), axis=(1, 2))
    win = np.swapaxes(h.reshape(B, NH, WS, NH, WS, C), 2, 3).reshape(-1, WS * WS, C)
    win = win
    qkv = (mxq(win, 2, "e4m3") @ mxq(f64(in_proj_w), 1, "e4m3").T) + f64(in_proj_b)
    q, k, v = np.split(qkv, 3, axis=-1)
    S, N = win.shape[0], win.shape[1]
    q = q.reshape(S, N, HEADS, HD) * (HD ** -0.5)
    k = k.reshape(S, N, HEADS, HD)
    v = v.reshape(S, N, HEADS, HD)
    return q, k, v

@@ -1,0 +1,277 @@
+from contextlib import ExitStack
+
+import concourse.mybir as mybir
+from concourse.masks import make_identity
+
+F32 = mybir.dt.float32
+BF16 = mybir.dt.bfloat16
+U32 = mybir.dt.uint32
+U8 = mybir.dt.uint8
+FP8X4 = mybir.dt.float8_e4m3fn_x4
+ALU = mybir.AluOpType
+ACT = mybir.ActivationFunctionType
+
+P = 128
+TOKENS = 1024
+CHANNELS = 1024
+OUT_COLS = 3072
+GRID = 32
+SHIFT = 4
+WINDOW = 8
+WINDOWS_IN_ROW = GRID // WINDOW
+GRID_ROWS_IN_TILE = P // GRID
+EPS = 1e-5
+Q_SCALE = 64 ** -0.5
+
+PACK = 4
+K_PASS = P * PACK
+PASSES = CHANNELS // K_PASS
+BANK = 512
+W_BLOCKS = OUT_COLS // BANK
+W_TILES = BANK // P
+X_TILES = TOKENS // P
+HALVES = 2
+HALF_TILES = X_TILES // HALVES
+PLANES = CHANNELS // P
+BN_CHUNK = 512
+PARTS = CHANNELS // BANK
+
+FLOPS = 2 * TOKENS * CHANNELS * OUT_COLS
+
+
+def tile_swintransformerblock_pa_kernel(
+    tc, x, ln1_w, ln1_b, in_proj_w, in_proj_b, out_0, out_1, out_2
+):
+    nc = tc.nc
+    x_rows = x.flatten_outer_dims()
+    out_rows = [o.rearrange("w n h d -> (w n) (h d)") for o in (out_0, out_1, out_2)]
+
+    with ExitStack() as stack:
+        const = stack.enter_context(tc.tile_pool(name="const", bufs=1))
+        keep = stack.enter_context(tc.tile_pool(name="keep", bufs=1))
+        small = stack.enter_context(tc.tile_pool(name="small", bufs=X_TILES))
+        normed = stack.enter_context(tc.tile_pool(name="normed", bufs=6))
+        group_h = stack.enter_context(tc.tile_pool(name="group_h", bufs=2))
+        group_w = stack.enter_context(tc.tile_pool(name="group_w", bufs=4))
+        results = stack.enter_context(tc.tile_pool(name="results", bufs=8))
+        psum = stack.enter_context(tc.psum_pool(name="psum", bufs=8))
+
+        x_sb = [keep.tile([P, CHANNELS], BF16, name="x_sb%d" % s) for s in range(X_TILES)]
+        w_raw = [keep.tile([P, W_TILES, CHANNELS], BF16, name="w_raw%d" % n) for n in range(W_BLOCKS)]
+
+        def source_tile(half, i):
+            return (half * HALF_TILES + i + 1) % X_TILES
+
+        def load_x(half):
+            for i in range(HALF_TILES):
+                s = source_tile(half, i)
+                nc.sync.dma_start(out=x_sb[s][:], in_=x_rows[s * P : (s + 1) * P, :])
+
+        def load_w(n):
+            rows = in_proj_w[n * BANK : (n + 1) * BANK, :]
+            nc.sync.dma_start(out=w_raw[n][:], in_=rows.rearrange("(a p) k -> p a k", p=P))
+
+        ln_gain_bf = const.tile([P, PASSES, PACK], BF16)
+        ln_bias_bf = const.tile([P, PASSES, PACK], BF16)
+        nc.scalar.dma_start(out=ln_gain_bf[:], in_=ln1_w.rearrange("(g p t) -> p g t", p=P, t=PACK))
+        nc.scalar.dma_start(out=ln_bias_bf[:], in_=ln1_b.rearrange("(g p t) -> p g t", p=P, t=PACK))
+
+        load_x(0)
+        load_w(0)
+        load_x(1)
+        load_w(1)
+        load_w(2)
+        bias = const.tile([P, OUT_COLS], BF16)
+        nc.sync.dma_start(out=bias[:], in_=in_proj_b.partition_broadcast(P))
+        for n in range(3, W_BLOCKS):
+            load_w(n)
+
+        eps = const.tile([P, 1], F32)
+        eps_rsqrt = const.tile([P, 1], F32)
+        nc.vector.memset(eps[:], EPS)
+        nc.scalar.activation(out=eps_rsqrt[:], in_=eps[:], func=ACT.Abs_reciprocal_sqrt)
+
+        ident = const.tile([P, P], F32)
+        make_identity(nc, ident[:])
+        ident_rows = ident[:].rearrange("p (i j) -> p i j", j=GRID)
+        rotated = const.tile([P, GRID_ROWS_IN_TILE, GRID], F32)
+        nc.vector.tensor_copy(out=rotated[:, :, 0 : GRID - SHIFT], in_=ident_rows[:, :, SHIFT:GRID])
+        nc.vector.tensor_copy(out=rotated[:, :, GRID - SHIFT : GRID], in_=ident_rows[:, :, 0:SHIFT])
+        perm = const.tile([P, WINDOWS_IN_ROW, GRID_ROWS_IN_TILE, WINDOW], F32)
+        nc.vector.tensor_copy(out=perm[:], in_=rotated[:].rearrange("p i (w c) -> p w i c", c=WINDOW))
+        perm_2d = perm[:].rearrange("p w i c -> p (w i c)")
+        ln_gain = const.tile([P, PASSES, PACK], F32)
+        ln_bias = const.tile([P, PASSES, PACK], F32)
+        nc.gpsimd.tensor_copy(out=ln_gain[:], in_=ln_gain_bf[:])
+        nc.gpsimd.tensor_copy(out=ln_bias[:], in_=ln_bias_bf[:])
+
+        def out_scale(n):
+            return Q_SCALE if n * BANK < CHANNELS else 1.0
+
+        h_codes = keep.tile([P, PASSES, TOKENS], U32, align_bytes=64)
+        h_scales = keep.tile([P, PASSES, TOKENS], U8, align_bytes=64)
+        w_codes = keep.tile([P, W_BLOCKS, PASSES, BANK], U32, align_bytes=64)
+        w_scales = keep.tile([P, W_BLOCKS, PASSES, BANK], U8, align_bytes=64)
+        planes = [keep.tile([P, PLANES, BANK], BF16, name="planes%d" % h) for h in range(HALVES)]
+        mean_var = {}
+        neg_mean = {}
+        xn = {}
+        grouped_w = {}
+
+        def tile_stats(s):
+            stats = small.tile([P, CHANNELS // BN_CHUNK, 6], F32, tag="stats")
+            for c in range(CHANNELS // BN_CHUNK):
+                nc.vector.bn_stats(out=stats[:, c, :], in_=x_sb[s][:, c * BN_CHUNK : (c + 1) * BN_CHUNK])
+            mean_var[s] = small.tile([P, 2], F32, name="mean_var", tag="mean_var")
+            nc.vector.bn_aggr(out=mean_var[s][:], in_=stats[:].rearrange("p c s -> p (c s)"))
+            neg_mean[s] = small.tile([P, 1], F32, name="neg_mean", tag="neg_mean")
+            nc.vector.tensor_scalar_mul(out=neg_mean[s][:], in0=mean_var[s][:, 0:1], scalar1=-1.0)
+
+        def tile_norm(s):
+            rstd = small.tile([P, 1], F32, tag="rstd")
+            nc.scalar.activation(
+                out=rstd[:], in_=mean_var[s][:, 1:2], func=ACT.Abs_reciprocal_sqrt, bias=eps[:, 0:1]
+            )
+            xn[s] = normed.tile([P, PACK, CHANNELS // PACK], F32, name="xn", tag="xn")
+            nc.gpsimd.tensor_scalar(
+                out=xn[s][:],
+                in0=x_sb[s][:].rearrange("p (w t) -> p t w", t=PACK),
+                scalar1=neg_mean[s][:, 0:1],
+                scalar2=rstd[:, 0:1],
+                op0=ALU.add,
+                op1=ALU.mult,
+            )
+
+        def turn_h(half, g):
+            for t in range(PACK):
+                turned = psum.tile([P, 2, WINDOWS_IN_ROW, 2, P // WINDOWS_IN_ROW], F32, tag="bank")
+                for i in range(HALF_TILES):
+                    wr, hb = divmod(i, 2)
+                    nc.tensor.transpose(
+                        out=turned[:, wr, :, hb, :],
+                        in_=xn[source_tile(half, i)][:, t, g * P : (g + 1) * P],
+                        identity=perm_2d,
+                    )
+                nc.scalar.activation(
+                    out=planes[half][:, PACK * g + t, :],
+                    in_=turned[:].rearrange("p a w b c -> p (a w b c)"),
+                    func=ACT.Identity,
+                    scale=ln_gain[:, g, t : t + 1],
+                    bias=ln_bias[:, g, t : t + 1],
+                )
+
+        def quantise_h(half, g):
+            rows = slice(half * BANK, (half + 1) * BANK)
+            grouped = group_h.tile([P, BANK, PACK], BF16, align_bytes=64, tag="grouped_h")
+            nc.vector.tensor_copy(
+                out=grouped[:].rearrange("p (c i) t -> p c t i", i=4),
+                in_=planes[half][:, PACK * g : PACK * (g + 1), :].rearrange("p t (c i) -> p c t i", i=4),
+            )
+            nc.vector.quantize_mx(
+                out=h_codes[:, g, rows].bitcast(FP8X4),
+                scales=h_scales[:, g, rows],
+                in_=grouped[:].rearrange("p c t -> p (c t)"),
+            )
+
+        def turn_w(n):
+            words = w_raw[n][:].bitcast(F32)
+            for g in range(PASSES):
+                grouped_w[n, g] = group_w.tile([P, BANK, PACK], BF16, align_bytes=64, name="grouped_w", tag="grouped_w")
+                grouped_words = grouped_w[n, g][:].bitcast(F32)
+                for pair in range(W_TILES // 2):
+                    turned = psum.tile([P, 2, 2, P], F32, tag="bank")
+                    for u in range(2):
+                        for a2 in range(2):
+                            first = 2 * g * P + u
+                            nc.tensor.transpose(
+                                out=turned[:, u, a2, :],
+                                in_=words[:, 2 * pair + a2, first : 2 * (g + 1) * P : 2],
+                                identity=ident[:],
+                            )
+                    nc.scalar.copy(
+                        out=grouped_words[:, 2 * pair * P : 2 * (pair + 1) * P, :],
+                        in_=turned[:].rearrange("p u a c -> p (a c) u"),
+                    )
+
+        def quantise_w(n):
+            for g in range(PASSES):
+                nc.vector.quantize_mx(
+                    out=w_codes[:, n, g, :].bitcast(FP8X4),
+                    scales=w_scales[:, n, g, :],
+                    in_=grouped_w[n, g][:].rearrange("p c t -> p (c t)"),
+                )
+
+        result_of = {}
+
+        def project(row_blocks, col_blocks):
+            pairs = [(m, n) for m in row_blocks for n in col_blocks]
+            accs = [psum.tile([P, BANK], F32, name="acc", tag="bank") for pair in pairs]
+            for g in range(PASSES):
+                for acc, (m, n) in zip(accs, pairs):
+                    rows = slice(m * P, (m + 1) * P)
+                    nc.tensor.matmul_mx(
+                        out=acc[:],
+                        lhsT=h_codes[:, g, rows].bitcast(FP8X4),
+                        lhsT_scale=h_scales[:, g, rows],
+                        rhs=w_codes[:, n, g, :].bitcast(FP8X4),
+                        rhs_scale=w_scales[:, n, g, :],
+                        start=(g == 0),
+                        stop=(g == PASSES - 1),
+                    )
+            for j, (m, n) in enumerate(pairs):
+                part = n % PARTS
+                if part == 0:
+                    result_of[m] = results.tile([P, CHANNELS], F32, name="result", tag="result")
+                result = result_of[m][:, part * BANK : (part + 1) * BANK]
+                cols = slice(n * BANK, (n + 1) * BANK)
+                if j == 0:
+                    nc.scalar.mul(out=result, in_=accs[j][:], mul=out_scale(n))
+                    nc.gpsimd.tensor_tensor(out=result, in0=result, in1=bias[:, cols], op=ALU.add)
+                else:
+                    nc.vector.scalar_tensor_tensor(
+                        out=result, in0=accs[j][:], scalar=out_scale(n), in1=bias[:, cols], op0=ALU.mult, op1=ALU.add
+                    )
+            complete = [(m, n // PARTS) for m, n in pairs if n % PARTS == PARTS - 1]
+            for m, which in complete[1:] + complete[:1]:
+                nc.sync.dma_start(out=out_rows[which][m * P : (m + 1) * P, :], in_=result_of[m][:])
+
+        for i in range(HALF_TILES):
+            tile_stats(source_tile(0, i))
+            tile_norm(source_tile(0, i))
+        turn_w(0)
+        tile_stats(source_tile(1, 0))
+        tile_stats(source_tile(1, 1))
+        quantise_w(0)
+        turn_h(0, 0)
+        tile_norm(source_tile(1, 0))
+        tile_norm(source_tile(1, 1))
+        tile_stats(source_tile(1, 2))
+        quantise_h(0, 0)
+        turn_h(0, 1)
+        tile_norm(source_tile(1, 2))
+        nc.gpsimd.tensor_scalar(
+            out=bias[:, 0:CHANNELS], in0=bias[:, 0:CHANNELS], scalar1=Q_SCALE, scalar2=0.0, op0=ALU.mult, op1=ALU.add
+        )
+        quantise_h(0, 1)
+        turn_w(1)
+        quantise_w(1)
+        turn_w(2)
+        rounds = [(which, m) for which in range(OUT_COLS // CHANNELS) for m in range(0, HALF_TILES, 2)]
+        later = [("w", 3), ("w", 4), ("w", 5), ("h", 0), ("h", 1)]
+        for i, (which, m) in enumerate(rounds):
+            project([m, m + 1], [PARTS * which, PARTS * which + 1])
+            if i == 0:
+                quantise_w(2)
+                tile_stats(source_tile(1, 3))
+                tile_norm(source_tile(1, 3))
+            if i < len(later):
+                kind, k = later[i]
+                if kind == "w":
+                    turn_w(k)
+                    quantise_w(k)
+                else:
+                    turn_h(1, k)
+                    quantise_h(1, k)
+        for which in range(OUT_COLS // CHANNELS):
+            for m in range(HALF_TILES, X_TILES, 2):
+                project([m, m + 1], [PARTS * which, PARTS * which + 1])

@@ -30,8 +30,9 @@ BANK = 512
 W_BLOCKS = OUT_COLS // BANK
 W_TILES = BANK // P
 X_TILES = TOKENS // P
-HALVES = 2
-HALF_TILES = X_TILES // HALVES
+QUARTERS = 4
+QUARTER_TILES = X_TILES // QUARTERS
+QUARTER = QUARTER_TILES * P
 PLANES = CHANNELS // P
 BN_CHUNK = 512
 PARTS = CHANNELS // BANK
@@ -51,7 +52,7 @@ def tile_swintransformerblock_pa_kernel(
         keep = stack.enter_context(tc.tile_pool(name="keep", bufs=1))
         small = stack.enter_context(tc.tile_pool(name="small", bufs=X_TILES))
         normed = stack.enter_context(tc.tile_pool(name="normed", bufs=6))
-        group_h = stack.enter_context(tc.tile_pool(name="group_h", bufs=2))
+        group_h = stack.enter_context(tc.tile_pool(name="group_h", bufs=4))
         group_w = stack.enter_context(tc.tile_pool(name="group_w", bufs=4))
         results = stack.enter_context(tc.tile_pool(name="results", bufs=8))
         psum = stack.enter_context(tc.psum_pool(name="psum", bufs=8))
@@ -59,32 +60,41 @@ def tile_swintransformerblock_pa_kernel(
         x_sb = [keep.tile([P, CHANNELS], BF16, name="x_sb%d" % s) for s in range(X_TILES)]
         w_raw = [keep.tile([P, W_TILES, CHANNELS], BF16, name="w_raw%d" % n) for n in range(W_BLOCKS)]
 
-        def source_tile(half, i):
-            return (half * HALF_TILES + i + 1) % X_TILES
+        def source_tile(q, i):
+            return (q * QUARTER_TILES + i + 1) % X_TILES
 
-        def load_x(half):
-            for i in range(HALF_TILES):
-                s = source_tile(half, i)
+        def load_x(q):
+            for i in range(QUARTER_TILES):
+                s = source_tile(q, i)
                 nc.sync.dma_start(out=x_sb[s][:], in_=x_rows[s * P : (s + 1) * P, :])
 
-        def load_w(n):
-            rows = in_proj_w[n * BANK : (n + 1) * BANK, :]
-            nc.sync.dma_start(out=w_raw[n][:], in_=rows.rearrange("(a p) k -> p a k", p=P))
+        def load_w(n, pair):
+            rows = in_proj_w[n * BANK + 2 * pair * P : n * BANK + 2 * (pair + 1) * P, :]
+            nc.sync.dma_start(
+                out=w_raw[n][:, 2 * pair : 2 * (pair + 1), :], in_=rows.rearrange("(a p) k -> p a k", p=P)
+            )
 
         ln_gain_bf = const.tile([P, PASSES, PACK], BF16)
         ln_bias_bf = const.tile([P, PASSES, PACK], BF16)
         nc.scalar.dma_start(out=ln_gain_bf[:], in_=ln1_w.rearrange("(g p t) -> p g t", p=P, t=PACK))
         nc.scalar.dma_start(out=ln_bias_bf[:], in_=ln1_b.rearrange("(g p t) -> p g t", p=P, t=PACK))
 
+        bias_row = const.tile([P, OUT_COLS], BF16)
+        nc.vector.memset(bias_row[:], 0.0)
+        load_w(0, 0)
         load_x(0)
-        load_w(0)
+        load_w(0, 1)
+        nc.scalar.dma_start(out=bias_row[0:1, :], in_=in_proj_b.rearrange("(o c) -> o c", o=1))
+        load_w(1, 0)
         load_x(1)
-        load_w(1)
-        load_w(2)
-        bias = const.tile([P, OUT_COLS], BF16)
-        nc.sync.dma_start(out=bias[:], in_=in_proj_b.partition_broadcast(P))
+        load_w(1, 1)
+        load_x(2)
+        load_w(2, 0)
+        load_w(2, 1)
+        load_x(3)
         for n in range(3, W_BLOCKS):
-            load_w(n)
+            load_w(n, 0)
+            load_w(n, 1)
 
         eps = const.tile([P, 1], F32)
         eps_rsqrt = const.tile([P, 1], F32)
@@ -105,6 +115,24 @@ def tile_swintransformerblock_pa_kernel(
         nc.gpsimd.tensor_copy(out=ln_gain[:], in_=ln_gain_bf[:])
         nc.gpsimd.tensor_copy(out=ln_bias[:], in_=ln_bias_bf[:])
 
+        bias = const.tile([P, OUT_COLS], BF16)
+        spread = const.tile([P, 2, P], BF16)
+        nc.vector.memset(spread[:, 0, :], Q_SCALE)
+        nc.vector.memset(spread[:, 1, :], 1.0)
+
+        def spread_bias(which):
+            turned = psum.tile([P, CHANNELS], BF16, tag="bank")
+            for part in range(PARTS):
+                first = which * CHANNELS + part * BANK
+                nc.tensor.matmul(
+                    out=turned[:, part * BANK : (part + 1) * BANK],
+                    lhsT=spread[:, min(which, 1), :],
+                    rhs=bias_row[:, first : first + BANK],
+                    start=True,
+                    stop=True,
+                )
+            nc.scalar.copy(out=bias[:, which * CHANNELS : (which + 1) * CHANNELS], in_=turned[:])
+
         def out_scale(n):
             return Q_SCALE if n * BANK < CHANNELS else 1.0
 
@@ -112,10 +140,11 @@ def tile_swintransformerblock_pa_kernel(
         h_scales = keep.tile([P, PASSES, TOKENS], U8, align_bytes=64)
         w_codes = keep.tile([P, W_BLOCKS, PASSES, BANK], U32, align_bytes=64)
         w_scales = keep.tile([P, W_BLOCKS, PASSES, BANK], U8, align_bytes=64)
-        planes = [keep.tile([P, PLANES, BANK], BF16, name="planes%d" % h) for h in range(HALVES)]
+        planes = [keep.tile([P, PLANES, QUARTER], BF16, name="planes%d" % q) for q in range(QUARTERS)]
         mean_var = {}
-        neg_mean = {}
+        rstd = {}
         xn = {}
+        grouped_h = {}
         grouped_w = {}
 
         def tile_stats(s):
@@ -124,82 +153,83 @@ def tile_swintransformerblock_pa_kernel(
                 nc.vector.bn_stats(out=stats[:, c, :], in_=x_sb[s][:, c * BN_CHUNK : (c + 1) * BN_CHUNK])
             mean_var[s] = small.tile([P, 2], F32, name="mean_var", tag="mean_var")
             nc.vector.bn_aggr(out=mean_var[s][:], in_=stats[:].rearrange("p c s -> p (c s)"))
-            neg_mean[s] = small.tile([P, 1], F32, name="neg_mean", tag="neg_mean")
-            nc.vector.tensor_scalar_mul(out=neg_mean[s][:], in0=mean_var[s][:, 0:1], scalar1=-1.0)
+
+        def tile_rstd(s):
+            rstd[s] = small.tile([P, 1], F32, name="rstd", tag="rstd")
+            nc.scalar.activation(
+                out=rstd[s][:], in_=mean_var[s][:, 1:2], func=ACT.Abs_reciprocal_sqrt, bias=eps[:, 0:1]
+            )
 
         def tile_norm(s):
-            rstd = small.tile([P, 1], F32, tag="rstd")
-            nc.scalar.activation(
-                out=rstd[:], in_=mean_var[s][:, 1:2], func=ACT.Abs_reciprocal_sqrt, bias=eps[:, 0:1]
-            )
             xn[s] = normed.tile([P, PACK, CHANNELS // PACK], F32, name="xn", tag="xn")
             nc.gpsimd.tensor_scalar(
                 out=xn[s][:],
                 in0=x_sb[s][:].rearrange("p (w t) -> p t w", t=PACK),
-                scalar1=neg_mean[s][:, 0:1],
-                scalar2=rstd[:, 0:1],
-                op0=ALU.add,
+                scalar1=mean_var[s][:, 0:1],
+                scalar2=rstd[s][:, 0:1],
+                op0=ALU.subtract,
                 op1=ALU.mult,
             )
 
-        def turn_h(half, g):
-            for t in range(PACK):
-                turned = psum.tile([P, 2, WINDOWS_IN_ROW, 2, P // WINDOWS_IN_ROW], F32, tag="bank")
-                for i in range(HALF_TILES):
-                    wr, hb = divmod(i, 2)
-                    nc.tensor.transpose(
-                        out=turned[:, wr, :, hb, :],
-                        in_=xn[source_tile(half, i)][:, t, g * P : (g + 1) * P],
-                        identity=perm_2d,
+        def turn_h(q, g):
+            for t0 in range(0, PACK, 2):
+                turned = psum.tile([P, 2, WINDOWS_IN_ROW, QUARTER_TILES, P // WINDOWS_IN_ROW], F32, tag="bank")
+                for t in (t0, t0 + 1):
+                    for hb in range(QUARTER_TILES):
+                        nc.tensor.transpose(
+                            out=turned[:, t - t0, :, hb, :],
+                            in_=xn[source_tile(q, hb)][:, t, g * P : (g + 1) * P],
+                            identity=perm_2d,
+                        )
+                for t in (t0, t0 + 1):
+                    nc.scalar.activation(
+                        out=planes[q][:, PACK * g + t, :],
+                        in_=turned[:, t - t0, :, :, :].rearrange("p w b c -> p (w b c)"),
+                        func=ACT.Identity,
+                        scale=ln_gain[:, g, t : t + 1],
+                        bias=ln_bias[:, g, t : t + 1],
                     )
-                nc.scalar.activation(
-                    out=planes[half][:, PACK * g + t, :],
-                    in_=turned[:].rearrange("p a w b c -> p (a w b c)"),
-                    func=ACT.Identity,
-                    scale=ln_gain[:, g, t : t + 1],
-                    bias=ln_bias[:, g, t : t + 1],
-                )
 
-        def quantise_h(half, g):
-            rows = slice(half * BANK, (half + 1) * BANK)
-            grouped = group_h.tile([P, BANK, PACK], BF16, align_bytes=64, tag="grouped_h")
+        def group_rows(q, g):
+            grouped_h[q, g] = group_h.tile([P, QUARTER, PACK], BF16, align_bytes=64, name="grouped_h", tag="grouped_h")
             nc.vector.tensor_copy(
-                out=grouped[:].rearrange("p (c i) t -> p c t i", i=4),
-                in_=planes[half][:, PACK * g : PACK * (g + 1), :].rearrange("p t (c i) -> p c t i", i=4),
+                out=grouped_h[q, g][:].rearrange("p (c i) t -> p c t i", i=4),
+                in_=planes[q][:, PACK * g : PACK * (g + 1), :].rearrange("p t (c i) -> p c t i", i=4),
             )
+
+        def quantise_h(q, g):
+            rows = slice(q * QUARTER, (q + 1) * QUARTER)
             nc.vector.quantize_mx(
                 out=h_codes[:, g, rows].bitcast(FP8X4),
                 scales=h_scales[:, g, rows],
-                in_=grouped[:].rearrange("p c t -> p (c t)"),
+                in_=grouped_h[q, g][:].rearrange("p c t -> p (c t)"),
             )
 
-        def turn_w(n):
+        def turn_w(n, pair):
             words = w_raw[n][:].bitcast(F32)
             for g in range(PASSES):
-                grouped_w[n, g] = group_w.tile([P, BANK, PACK], BF16, align_bytes=64, name="grouped_w", tag="grouped_w")
-                grouped_words = grouped_w[n, g][:].bitcast(F32)
-                for pair in range(W_TILES // 2):
-                    turned = psum.tile([P, 2, 2, P], F32, tag="bank")
-                    for u in range(2):
-                        for a2 in range(2):
-                            first = 2 * g * P + u
-                            nc.tensor.transpose(
-                                out=turned[:, u, a2, :],
-                                in_=words[:, 2 * pair + a2, first : 2 * (g + 1) * P : 2],
-                                identity=ident[:],
-                            )
-                    nc.scalar.copy(
-                        out=grouped_words[:, 2 * pair * P : 2 * (pair + 1) * P, :],
-                        in_=turned[:].rearrange("p u a c -> p (a c) u"),
-                    )
-
-        def quantise_w(n):
-            for g in range(PASSES):
-                nc.vector.quantize_mx(
-                    out=w_codes[:, n, g, :].bitcast(FP8X4),
-                    scales=w_scales[:, n, g, :],
-                    in_=grouped_w[n, g][:].rearrange("p c t -> p (c t)"),
+                if pair == 0:
+                    grouped_w[n, g] = group_w.tile([P, BANK, PACK], BF16, align_bytes=64, name="grouped_w", tag="grouped_w")
+                turned = psum.tile([P, 2, 2, P], F32, tag="bank")
+                for u in range(2):
+                    for a2 in range(2):
+                        first = 2 * g * P + u
+                        nc.tensor.transpose(
+                            out=turned[:, u, a2, :],
+                            in_=words[:, 2 * pair + a2, first : 2 * (g + 1) * P : 2],
+                            identity=ident[:],
+                        )
+                nc.scalar.copy(
+                    out=grouped_w[n, g][:].bitcast(F32)[:, 2 * pair * P : 2 * (pair + 1) * P, :],
+                    in_=turned[:].rearrange("p u a c -> p (a c) u"),
                 )
+
+        def quantise_w(n, g):
+            nc.vector.quantize_mx(
+                out=w_codes[:, n, g, :].bitcast(FP8X4),
+                scales=w_scales[:, n, g, :],
+                in_=grouped_w[n, g][:].rearrange("p c t -> p (c t)"),
+            )
 
         result_of = {}
 
@@ -235,43 +265,73 @@ def tile_swintransformerblock_pa_kernel(
             for m, which in complete[1:] + complete[:1]:
                 nc.sync.dma_start(out=out_rows[which][m * P : (m + 1) * P, :], in_=result_of[m][:])
 
-        for i in range(HALF_TILES):
-            tile_stats(source_tile(0, i))
-            tile_norm(source_tile(0, i))
-        turn_w(0)
-        tile_stats(source_tile(1, 0))
-        tile_stats(source_tile(1, 1))
-        quantise_w(0)
-        turn_h(0, 0)
-        tile_norm(source_tile(1, 0))
-        tile_norm(source_tile(1, 1))
-        tile_stats(source_tile(1, 2))
-        quantise_h(0, 0)
-        turn_h(0, 1)
-        tile_norm(source_tile(1, 2))
-        nc.gpsimd.tensor_scalar(
-            out=bias[:, 0:CHANNELS], in0=bias[:, 0:CHANNELS], scalar1=Q_SCALE, scalar2=0.0, op0=ALU.mult, op1=ALU.add
-        )
-        quantise_h(0, 1)
-        turn_w(1)
-        quantise_w(1)
-        turn_w(2)
-        rounds = [(which, m) for which in range(OUT_COLS // CHANNELS) for m in range(0, HALF_TILES, 2)]
-        later = [("w", 3), ("w", 4), ("w", 5), ("h", 0), ("h", 1)]
-        for i, (which, m) in enumerate(rounds):
-            project([m, m + 1], [PARTS * which, PARTS * which + 1])
-            if i == 0:
-                quantise_w(2)
-                tile_stats(source_tile(1, 3))
-                tile_norm(source_tile(1, 3))
-            if i < len(later):
-                kind, k = later[i]
-                if kind == "w":
-                    turn_w(k)
-                    quantise_w(k)
-                else:
-                    turn_h(1, k)
-                    quantise_h(1, k)
-        for which in range(OUT_COLS // CHANNELS):
-            for m in range(HALF_TILES, X_TILES, 2):
-                project([m, m + 1], [PARTS * which, PARTS * which + 1])
+        def tiles(q):
+            return [source_tile(q, i) for i in range(QUARTER_TILES)]
+
+        def stats(q):
+            for s in tiles(q):
+                tile_stats(s)
+
+        def roots(q):
+            for s in tiles(q):
+                tile_rstd(s)
+
+        def norm(q):
+            for s in tiles(q):
+                tile_norm(s)
+
+        def turn_rows(q):
+            for g in range(PASSES):
+                turn_h(q, g)
+
+        def quantise_rows(q):
+            group_rows(q, 0)
+            group_rows(q, 1)
+            quantise_h(q, 0)
+            quantise_h(q, 1)
+
+        def prepare_w(n):
+            for g in range(PASSES):
+                quantise_w(n, g)
+
+        def project_rows(q, which):
+            project([2 * q, 2 * q + 1], [PARTS * which, PARTS * which + 1])
+
+        for s in tiles(0):
+            tile_stats(s)
+            tile_rstd(s)
+            tile_norm(s)
+        turn_w(0, 0)
+        stats(1)
+        spread_bias(0)
+        turn_w(0, 1)
+        roots(1)
+        norm(1)
+        turn_rows(0)
+        prepare_w(0)
+        quantise_rows(0)
+        turn_w(1, 0)
+        turn_w(1, 1)
+        stats(2)
+        roots(2)
+        norm(2)
+        turn_rows(1)
+        prepare_w(1)
+        for q in range(QUARTERS):
+            turn_w(q + 2, 0)
+            if q + 1 < QUARTERS:
+                quantise_rows(q + 1)
+            if q + 3 < QUARTERS:
+                stats(q + 3)
+                roots(q + 3)
+                norm(q + 3)
+            project_rows(q, 0)
+            turn_w(q + 2, 1)
+            if q + 2 < QUARTERS:
+                turn_rows(q + 2)
+            prepare_w(q + 2)
+            if q < 2:
+                spread_bias(q + 1)
+        for which in range(1, OUT_COLS // CHANNELS):
+            for q in range(QUARTERS):
+                project_rows(q, which)

@@ -142,6 +142,7 @@ def tile_swintransformerblock_pa_kernel(
         w_scales = keep.tile([P, W_BLOCKS, PASSES, BANK], U8, align_bytes=64)
         planes = [keep.tile([P, PLANES, QUARTER], BF16, name="planes%d" % q) for q in range(QUARTERS)]
         mean_var = {}
+        neg_mean = {}
         rstd = {}
         xn = {}
         grouped_h = {}
@@ -155,6 +156,8 @@ def tile_swintransformerblock_pa_kernel(
             nc.vector.bn_aggr(out=mean_var[s][:], in_=stats[:].rearrange("p c s -> p (c s)"))
 
         def tile_rstd(s):
+            neg_mean[s] = small.tile([P, 1], F32, name="neg_mean", tag="neg_mean")
+            nc.scalar.mul(out=neg_mean[s][:], in_=mean_var[s][:, 0:1], mul=-1.0)
             rstd[s] = small.tile([P, 1], F32, name="rstd", tag="rstd")
             nc.scalar.activation(
                 out=rstd[s][:], in_=mean_var[s][:, 1:2], func=ACT.Abs_reciprocal_sqrt, bias=eps[:, 0:1]
@@ -165,9 +168,9 @@ def tile_swintransformerblock_pa_kernel(
             nc.gpsimd.tensor_scalar(
                 out=xn[s][:],
                 in0=x_sb[s][:].rearrange("p (w t) -> p t w", t=PACK),
-                scalar1=mean_var[s][:, 0:1],
+                scalar1=neg_mean[s][:, 0:1],
                 scalar2=rstd[s][:, 0:1],
-                op0=ALU.subtract,
+                op0=ALU.add,
                 op1=ALU.mult,
             )
 

@@ -7,6 +7,7 @@ F32 = mybir.dt.float32
 BF16 = mybir.dt.bfloat16
 U32 = mybir.dt.uint32
 U8 = mybir.dt.uint8
+I32 = mybir.dt.int32
 FP8X4 = mybir.dt.float8_e4m3fn_x4
 ALU = mybir.AluOpType
 ACT = mybir.ActivationFunctionType
@@ -51,7 +52,7 @@ def tile_swintransformerblock_pa_kernel(
         const = stack.enter_context(tc.tile_pool(name="const", bufs=1))
         keep = stack.enter_context(tc.tile_pool(name="keep", bufs=1))
         small = stack.enter_context(tc.tile_pool(name="small", bufs=X_TILES))
-        normed = stack.enter_context(tc.tile_pool(name="normed", bufs=6))
+        normed = stack.enter_context(tc.tile_pool(name="normed", bufs=8))
         group_h = stack.enter_context(tc.tile_pool(name="group_h", bufs=4))
         group_w = stack.enter_context(tc.tile_pool(name="group_w", bufs=4))
         results = stack.enter_context(tc.tile_pool(name="results", bufs=8))
@@ -74,60 +75,67 @@ def tile_swintransformerblock_pa_kernel(
                 out=w_raw[n][:, 2 * pair : 2 * (pair + 1), :], in_=rows.rearrange("(a p) k -> p a k", p=P)
             )
 
+        bias_rows = const.tile([P, BANK], BF16)
+        nc.vector.memset(bias_rows[:].bitcast(I32), 0)
+        b_rows = in_proj_b.rearrange("(r c) -> r c", c=BANK)
         ln_gain_bf = const.tile([P, PASSES, PACK], BF16)
         ln_bias_bf = const.tile([P, PASSES, PACK], BF16)
         nc.scalar.dma_start(out=ln_gain_bf[:], in_=ln1_w.rearrange("(g p t) -> p g t", p=P, t=PACK))
         nc.scalar.dma_start(out=ln_bias_bf[:], in_=ln1_b.rearrange("(g p t) -> p g t", p=P, t=PACK))
-
-        bias_row = const.tile([P, OUT_COLS], BF16)
-        nc.vector.memset(bias_row[:], 0.0)
-        load_w(0, 0)
-        load_x(0)
-        load_w(0, 1)
-        nc.scalar.dma_start(out=bias_row[0:1, :], in_=in_proj_b.rearrange("(o c) -> o c", o=1))
-        load_w(1, 0)
-        load_x(1)
-        load_w(1, 1)
-        load_x(2)
-        load_w(2, 0)
-        load_w(2, 1)
-        load_x(3)
-        for n in range(3, W_BLOCKS):
-            load_w(n, 0)
-            load_w(n, 1)
+        nc.scalar.dma_start(out=bias_rows[0:4, :], in_=b_rows[0:4, :])
+        nc.scalar.dma_start(out=bias_rows[4:W_BLOCKS, :], in_=b_rows[4:W_BLOCKS, :])
 
         eps = const.tile([P, 1], F32)
         eps_rsqrt = const.tile([P, 1], F32)
         nc.vector.memset(eps[:], EPS)
         nc.scalar.activation(out=eps_rsqrt[:], in_=eps[:], func=ACT.Abs_reciprocal_sqrt)
 
+
+        load_w(0, 0)
+        load_x(0)
+        load_w(0, 1)
+        load_x(1)
+        load_w(1, 0)
+        load_x(2)
+        load_w(1, 1)
+        load_x(3)
+        load_w(2, 0)
+        load_w(2, 1)
+        load_w(3, 0)
+        load_w(3, 1)
+        load_w(4, 0)
+        load_w(4, 1)
+        load_w(5, 0)
+        load_w(5, 1)
         ident = const.tile([P, P], F32)
         make_identity(nc, ident[:])
         ident_rows = ident[:].rearrange("p (i j) -> p i j", j=GRID)
         rotated = const.tile([P, GRID_ROWS_IN_TILE, GRID], F32)
-        nc.vector.tensor_copy(out=rotated[:, :, 0 : GRID - SHIFT], in_=ident_rows[:, :, SHIFT:GRID])
-        nc.vector.tensor_copy(out=rotated[:, :, GRID - SHIFT : GRID], in_=ident_rows[:, :, 0:SHIFT])
+        nc.gpsimd.tensor_copy(out=rotated[:, :, 0 : GRID - SHIFT], in_=ident_rows[:, :, SHIFT:GRID])
+        nc.gpsimd.tensor_copy(out=rotated[:, :, GRID - SHIFT : GRID], in_=ident_rows[:, :, 0:SHIFT])
         perm = const.tile([P, WINDOWS_IN_ROW, GRID_ROWS_IN_TILE, WINDOW], F32)
-        nc.vector.tensor_copy(out=perm[:], in_=rotated[:].rearrange("p i (w c) -> p w i c", c=WINDOW))
+        nc.gpsimd.tensor_copy(out=perm[:], in_=rotated[:].rearrange("p i (w c) -> p w i c", c=WINDOW))
         perm_2d = perm[:].rearrange("p w i c -> p (w i c)")
+        bias = const.tile([P, OUT_COLS], BF16)
+        pick = const.tile([P, W_BLOCKS], BF16)
+        nc.gpsimd.tensor_scalar(
+            out=pick[:, 0:PARTS], in0=ident[:, 0:PARTS], scalar1=Q_SCALE, scalar2=0.0, op0=ALU.mult, op1=ALU.add
+        )
+        nc.gpsimd.tensor_copy(out=pick[:, PARTS:W_BLOCKS], in_=ident[:, PARTS:W_BLOCKS])
+
         ln_gain = const.tile([P, PASSES, PACK], F32)
         ln_bias = const.tile([P, PASSES, PACK], F32)
         nc.gpsimd.tensor_copy(out=ln_gain[:], in_=ln_gain_bf[:])
         nc.gpsimd.tensor_copy(out=ln_bias[:], in_=ln_bias_bf[:])
 
-        bias = const.tile([P, OUT_COLS], BF16)
-        spread = const.tile([P, 2, P], BF16)
-        nc.vector.memset(spread[:, 0, :], Q_SCALE)
-        nc.vector.memset(spread[:, 1, :], 1.0)
-
         def spread_bias(which):
             turned = psum.tile([P, CHANNELS], BF16, tag="bank")
             for part in range(PARTS):
-                first = which * CHANNELS + part * BANK
+                n = which * PARTS + part
                 nc.tensor.matmul(
                     out=turned[:, part * BANK : (part + 1) * BANK],
-                    lhsT=spread[:, min(which, 1), :],
-                    rhs=bias_row[:, first : first + BANK],
+                    lhsT=pick[:, n : n + 1].to_broadcast([P, P]),
+                    rhs=bias_rows[:],
                     start=True,
                     stop=True,
                 )
@@ -234,14 +242,12 @@ def tile_swintransformerblock_pa_kernel(
                 in_=grouped_w[n, g][:].rearrange("p c t -> p (c t)"),
             )
 
-        result_of = {}
-
-        def project(row_blocks, col_blocks):
-            pairs = [(m, n) for m in row_blocks for n in col_blocks]
-            accs = [psum.tile([P, BANK], F32, name="acc", tag="bank") for pair in pairs]
-            for g in range(PASSES):
-                for acc, (m, n) in zip(accs, pairs):
-                    rows = slice(m * P, (m + 1) * P)
+        def project(m, which, banks_of_scalar, stores):
+            rows = slice(m * P, (m + 1) * P)
+            blocks = range(PARTS * which, PARTS * (which + 1))
+            accs = [psum.tile([P, BANK], F32, name="acc", tag="bank") for n in blocks]
+            for acc, n in zip(accs, blocks):
+                for g in range(PASSES):
                     nc.tensor.matmul_mx(
                         out=acc[:],
                         lhsT=h_codes[:, g, rows].bitcast(FP8X4),
@@ -251,90 +257,143 @@ def tile_swintransformerblock_pa_kernel(
                         start=(g == 0),
                         stop=(g == PASSES - 1),
                     )
-            for j, (m, n) in enumerate(pairs):
-                part = n % PARTS
-                if part == 0:
-                    result_of[m] = results.tile([P, CHANNELS], F32, name="result", tag="result")
-                result = result_of[m][:, part * BANK : (part + 1) * BANK]
+            result = results.tile([P, CHANNELS], F32, name="result", tag="result")
+            for j, (acc, n) in enumerate(zip(accs, blocks)):
+                piece = result[:, j * BANK : (j + 1) * BANK]
                 cols = slice(n * BANK, (n + 1) * BANK)
-                if j == 0:
-                    nc.scalar.mul(out=result, in_=accs[j][:], mul=out_scale(n))
-                    nc.gpsimd.tensor_tensor(out=result, in0=result, in1=bias[:, cols], op=ALU.add)
+                if j < banks_of_scalar:
+                    nc.scalar.mul(out=piece, in_=acc[:], mul=out_scale(n))
+                    nc.gpsimd.tensor_tensor(out=piece, in0=piece, in1=bias[:, cols], op=ALU.add)
                 else:
                     nc.vector.scalar_tensor_tensor(
-                        out=result, in0=accs[j][:], scalar=out_scale(n), in1=bias[:, cols], op0=ALU.mult, op1=ALU.add
+                        out=piece, in0=acc[:], scalar=out_scale(n), in1=bias[:, cols], op0=ALU.mult, op1=ALU.add
                     )
-            complete = [(m, n // PARTS) for m, n in pairs if n % PARTS == PARTS - 1]
-            for m, which in complete[1:] + complete[:1]:
-                nc.sync.dma_start(out=out_rows[which][m * P : (m + 1) * P, :], in_=result_of[m][:])
+            width = CHANNELS // stores
+            for c in range(stores):
+                cols = slice(c * width, (c + 1) * width)
+                nc.sync.dma_start(out=out_rows[which][rows, cols], in_=result[:, cols])
 
-        def tiles(q):
-            return [source_tile(q, i) for i in range(QUARTER_TILES)]
-
-        def stats(q):
-            for s in tiles(q):
-                tile_stats(s)
-
-        def roots(q):
-            for s in tiles(q):
-                tile_rstd(s)
-
-        def norm(q):
-            for s in tiles(q):
-                tile_norm(s)
-
-        def turn_rows(q):
-            for g in range(PASSES):
-                turn_h(q, g)
-
-        def quantise_rows(q):
-            group_rows(q, 0)
-            group_rows(q, 1)
-            quantise_h(q, 0)
-            quantise_h(q, 1)
-
-        def prepare_w(n):
-            for g in range(PASSES):
-                quantise_w(n, g)
-
-        def project_rows(q, which):
-            project([2 * q, 2 * q + 1], [PARTS * which, PARTS * which + 1])
-
-        for s in tiles(0):
-            tile_stats(s)
-            tile_rstd(s)
-            tile_norm(s)
-        turn_w(0, 0)
-        stats(1)
-        spread_bias(0)
-        turn_w(0, 1)
-        roots(1)
-        norm(1)
-        turn_rows(0)
-        prepare_w(0)
-        quantise_rows(0)
-        turn_w(1, 0)
-        turn_w(1, 1)
-        stats(2)
-        roots(2)
-        norm(2)
-        turn_rows(1)
-        prepare_w(1)
-        for q in range(QUARTERS):
-            turn_w(q + 2, 0)
-            if q + 1 < QUARTERS:
-                quantise_rows(q + 1)
-            if q + 3 < QUARTERS:
-                stats(q + 3)
-                roots(q + 3)
-                norm(q + 3)
-            project_rows(q, 0)
-            turn_w(q + 2, 1)
-            if q + 2 < QUARTERS:
-                turn_rows(q + 2)
-            prepare_w(q + 2)
-            if q < 2:
-                spread_bias(q + 1)
-        for which in range(1, OUT_COLS // CHANNELS):
-            for q in range(QUARTERS):
-                project_rows(q, which)
+        def st(q):
+            for i in range(QUARTER_TILES):
+                tile_stats(source_tile(q, i))
+        def rt(q):
+            for i in range(QUARTER_TILES):
+                tile_rstd(source_tile(q, i))
+        def nm(q):
+            for i in range(QUARTER_TILES):
+                tile_norm(source_tile(q, i))
+        def sn(q):
+            for i in range(QUARTER_TILES):
+                tile_stats(source_tile(q, i))
+                tile_rstd(source_tile(q, i))
+                tile_norm(source_tile(q, i))
+        def s1(q, i):
+            tile_stats(source_tile(q, i))
+        def r1(q, i):
+            tile_rstd(source_tile(q, i))
+        def n1(q, i):
+            tile_norm(source_tile(q, i))
+        tx, ih, qh, tw, qw, bs = turn_h, group_rows, quantise_h, turn_w, quantise_w, spread_bias
+        def pj(m, which, k=-1):
+            last = which == 2 and m >= 6
+            project(m, which, k if k >= 0 else 0 if last else m % 2, 2 if last else 1)
+        with tc.manual_schedule():
+            tw(0, 0)
+            s1(0, 0)
+            s1(0, 1)
+            r1(0, 0)
+            r1(0, 1)
+            n1(0, 0)
+            n1(0, 1)
+            tw(0, 1)
+            s1(1, 0)
+            s1(1, 1)
+            tw(1, 0)
+            r1(1, 0)
+            r1(1, 1)
+            n1(1, 0)
+            n1(1, 1)
+            tx(0, 0)
+            tx(0, 1)
+            s1(2, 0)
+            s1(2, 1)
+            bs(0)
+            tw(1, 1)
+            r1(2, 0)
+            r1(2, 1)
+            n1(2, 0)
+            n1(2, 1)
+            tx(1, 0)
+            s1(3, 0)
+            s1(3, 1)
+            qw(0, 0)
+            qw(0, 1)
+            ih(0, 0)
+            ih(0, 1)
+            tw(2, 0)
+            r1(3, 0)
+            r1(3, 1)
+            n1(3, 0)
+            n1(3, 1)
+            qh(0, 0)
+            qh(0, 1)
+            tx(1, 1)
+            qw(1, 0)
+            qw(1, 1)
+            tw(2, 1)
+            pj(0, 0)
+            pj(1, 0)
+            ih(1, 0)
+            ih(1, 1)
+            qh(1, 0)
+            qh(1, 1)
+            tw(3, 0)
+            bs(1)
+            qw(2, 0)
+            qw(2, 1)
+            tx(2, 0)
+            tx(2, 1)
+            pj(2, 0)
+            pj(3, 0)
+            tw(3, 1)
+            bs(2)
+            qw(3, 0)
+            qw(3, 1)
+            pj(0, 1)
+            pj(1, 1)
+            ih(2, 0)
+            ih(2, 1)
+            qh(2, 0)
+            qh(2, 1)
+            tx(3, 0)
+            tx(3, 1)
+            pj(2, 1)
+            pj(3, 1)
+            tw(4, 0)
+            tw(4, 1)
+            pj(4, 0)
+            pj(5, 0)
+            ih(3, 0)
+            ih(3, 1)
+            qh(3, 0)
+            qh(3, 1)
+            qw(4, 0)
+            qw(4, 1)
+            pj(4, 1)
+            pj(5, 1)
+            tw(5, 0)
+            tw(5, 1)
+            pj(6, 0)
+            pj(7, 0)
+            qw(5, 0)
+            qw(5, 1)
+            pj(6, 1)
+            pj(7, 1)
+            pj(0, 2)
+            pj(1, 2)
+            pj(2, 2)
+            pj(3, 2)
+            pj(4, 2)
+            pj(5, 2)
+            pj(6, 2)
+            pj(7, 2)

@@ -52,7 +52,7 @@ def tile_swintransformerblock_pa_kernel(
         const = stack.enter_context(tc.tile_pool(name="const", bufs=1))
         keep = stack.enter_context(tc.tile_pool(name="keep", bufs=1))
         small = stack.enter_context(tc.tile_pool(name="small", bufs=X_TILES))
-        normed = stack.enter_context(tc.tile_pool(name="normed", bufs=8))
+        normed = stack.enter_context(tc.tile_pool(name="normed", bufs=X_TILES))
         group_h = stack.enter_context(tc.tile_pool(name="group_h", bufs=4))
         group_w = stack.enter_context(tc.tile_pool(name="group_w", bufs=4))
         results = stack.enter_context(tc.tile_pool(name="results", bufs=8))
@@ -64,49 +64,49 @@ def tile_swintransformerblock_pa_kernel(
         def source_tile(q, i):
             return (q * QUARTER_TILES + i + 1) % X_TILES
 
-        def load_x(q):
-            for i in range(QUARTER_TILES):
-                s = source_tile(q, i)
-                nc.sync.dma_start(out=x_sb[s][:], in_=x_rows[s * P : (s + 1) * P, :])
+        def load_x(q, i):
+            s = source_tile(q, i)
+            nc.sync.dma_start(out=x_sb[s][:], in_=x_rows[s * P : (s + 1) * P, :])
 
-        def load_w(n, pair):
-            rows = in_proj_w[n * BANK + 2 * pair * P : n * BANK + 2 * (pair + 1) * P, :]
+        def load_w(n, first, tiles):
+            rows = in_proj_w[n * BANK + first * P : n * BANK + (first + tiles) * P, :]
             nc.sync.dma_start(
-                out=w_raw[n][:, 2 * pair : 2 * (pair + 1), :], in_=rows.rearrange("(a p) k -> p a k", p=P)
+                out=w_raw[n][:, first : first + tiles, :], in_=rows.rearrange("(a p) k -> p a k", p=P)
             )
 
         bias_rows = const.tile([P, BANK], BF16)
         nc.vector.memset(bias_rows[:].bitcast(I32), 0)
-        b_rows = in_proj_b.rearrange("(r c) -> r c", c=BANK)
         ln_gain_bf = const.tile([P, PASSES, PACK], BF16)
         ln_bias_bf = const.tile([P, PASSES, PACK], BF16)
         nc.scalar.dma_start(out=ln_gain_bf[:], in_=ln1_w.rearrange("(g p t) -> p g t", p=P, t=PACK))
         nc.scalar.dma_start(out=ln_bias_bf[:], in_=ln1_b.rearrange("(g p t) -> p g t", p=P, t=PACK))
-        nc.scalar.dma_start(out=bias_rows[0:4, :], in_=b_rows[0:4, :])
-        nc.scalar.dma_start(out=bias_rows[4:W_BLOCKS, :], in_=b_rows[4:W_BLOCKS, :])
+        nc.scalar.dma_start(out=bias_rows[0:PARTS, :], in_=in_proj_b[0:CHANNELS].rearrange("(r c) -> r c", c=BANK))
 
         eps = const.tile([P, 1], F32)
         eps_rsqrt = const.tile([P, 1], F32)
         nc.vector.memset(eps[:], EPS)
         nc.scalar.activation(out=eps_rsqrt[:], in_=eps[:], func=ACT.Abs_reciprocal_sqrt)
 
+        for i in range(QUARTER_TILES):
+            load_x(0, i)
+            load_w(0, i, 1)
+        for i in range(QUARTER_TILES):
+            load_x(1, i)
+        load_w(0, W_TILES // 2, W_TILES // 2)
+        for half in range(2):
+            load_w(1, half * W_TILES // 2, W_TILES // 2)
+            load_x(2, half)
+        for n in range(2, W_BLOCKS):
+            for half in range(2):
+                load_w(n, half * W_TILES // 2, W_TILES // 2)
+            if n == 2:
+                for i in range(QUARTER_TILES):
+                    load_x(3, i)
+        bias = const.tile([P, OUT_COLS], BF16)
+        for which in range(1, OUT_COLS // CHANNELS):
+            cols = slice(which * CHANNELS, (which + 1) * CHANNELS)
+            nc.sync.dma_start(out=bias[:, cols], in_=in_proj_b[cols].partition_broadcast(P))
 
-        load_w(0, 0)
-        load_x(0)
-        load_w(0, 1)
-        load_x(1)
-        load_w(1, 0)
-        load_x(2)
-        load_w(1, 1)
-        load_x(3)
-        load_w(2, 0)
-        load_w(2, 1)
-        load_w(3, 0)
-        load_w(3, 1)
-        load_w(4, 0)
-        load_w(4, 1)
-        load_w(5, 0)
-        load_w(5, 1)
         ident = const.tile([P, P], F32)
         make_identity(nc, ident[:])
         ident_rows = ident[:].rearrange("p (i j) -> p i j", j=GRID)
@@ -116,30 +116,26 @@ def tile_swintransformerblock_pa_kernel(
         perm = const.tile([P, WINDOWS_IN_ROW, GRID_ROWS_IN_TILE, WINDOW], F32)
         nc.gpsimd.tensor_copy(out=perm[:], in_=rotated[:].rearrange("p i (w c) -> p w i c", c=WINDOW))
         perm_2d = perm[:].rearrange("p w i c -> p (w i c)")
-        bias = const.tile([P, OUT_COLS], BF16)
-        pick = const.tile([P, W_BLOCKS], BF16)
+        pick = const.tile([P, PARTS], BF16)
         nc.gpsimd.tensor_scalar(
-            out=pick[:, 0:PARTS], in0=ident[:, 0:PARTS], scalar1=Q_SCALE, scalar2=0.0, op0=ALU.mult, op1=ALU.add
+            out=pick[:], in0=ident[:, 0:PARTS], scalar1=Q_SCALE, scalar2=0.0, op0=ALU.mult, op1=ALU.add
         )
-        nc.gpsimd.tensor_copy(out=pick[:, PARTS:W_BLOCKS], in_=ident[:, PARTS:W_BLOCKS])
-
         ln_gain = const.tile([P, PASSES, PACK], F32)
         ln_bias = const.tile([P, PASSES, PACK], F32)
         nc.gpsimd.tensor_copy(out=ln_gain[:], in_=ln_gain_bf[:])
         nc.gpsimd.tensor_copy(out=ln_bias[:], in_=ln_bias_bf[:])
 
-        def spread_bias(which):
-            turned = psum.tile([P, CHANNELS], BF16, tag="bank")
-            for part in range(PARTS):
-                n = which * PARTS + part
+        def spread_bias():
+            spread = psum.tile([P, CHANNELS], BF16, tag="bank")
+            for r in range(PARTS):
                 nc.tensor.matmul(
-                    out=turned[:, part * BANK : (part + 1) * BANK],
-                    lhsT=pick[:, n : n + 1].to_broadcast([P, P]),
+                    out=spread[:, r * BANK : (r + 1) * BANK],
+                    lhsT=pick[:, r : r + 1].to_broadcast([P, P]),
                     rhs=bias_rows[:],
                     start=True,
                     stop=True,
                 )
-            nc.scalar.copy(out=bias[:, which * CHANNELS : (which + 1) * CHANNELS], in_=turned[:])
+            nc.scalar.copy(out=bias[:, 0:CHANNELS], in_=spread[:])
 
         def out_scale(n):
             return Q_SCALE if n * BANK < CHANNELS else 1.0
@@ -165,7 +161,9 @@ def tile_swintransformerblock_pa_kernel(
 
         def tile_rstd(s):
             neg_mean[s] = small.tile([P, 1], F32, name="neg_mean", tag="neg_mean")
-            nc.scalar.mul(out=neg_mean[s][:], in_=mean_var[s][:, 0:1], mul=-1.0)
+            nc.gpsimd.tensor_scalar(
+                out=neg_mean[s][:], in0=mean_var[s][:, 0:1], scalar1=-1.0, scalar2=0.0, op0=ALU.mult, op1=ALU.add
+            )
             rstd[s] = small.tile([P, 1], F32, name="rstd", tag="rstd")
             nc.scalar.activation(
                 out=rstd[s][:], in_=mean_var[s][:, 1:2], func=ACT.Abs_reciprocal_sqrt, bias=eps[:, 0:1]
@@ -273,127 +271,64 @@ def tile_swintransformerblock_pa_kernel(
                 cols = slice(c * width, (c + 1) * width)
                 nc.sync.dma_start(out=out_rows[which][rows, cols], in_=result[:, cols])
 
-        def st(q):
-            for i in range(QUARTER_TILES):
-                tile_stats(source_tile(q, i))
-        def rt(q):
-            for i in range(QUARTER_TILES):
-                tile_rstd(source_tile(q, i))
-        def nm(q):
-            for i in range(QUARTER_TILES):
-                tile_norm(source_tile(q, i))
-        def sn(q):
-            for i in range(QUARTER_TILES):
-                tile_stats(source_tile(q, i))
-                tile_rstd(source_tile(q, i))
-                tile_norm(source_tile(q, i))
-        def s1(q, i):
-            tile_stats(source_tile(q, i))
-        def r1(q, i):
-            tile_rstd(source_tile(q, i))
-        def n1(q, i):
-            tile_norm(source_tile(q, i))
-        tx, ih, qh, tw, qw, bs = turn_h, group_rows, quantise_h, turn_w, quantise_w, spread_bias
-        def pj(m, which, k=-1):
-            last = which == 2 and m >= 6
-            project(m, which, k if k >= 0 else 0 if last else m % 2, 2 if last else 1)
+        units = [("w", 0), ("x", 0), ("w", 1), ("x", 1), ("w", 2), ("x", 2), ("w", 3), ("x", 3), ("w", 4), ("w", 5)]
+        ahead, behind, projected = 3, 2, 3
+
+        def statistics(unit, half):
+            if unit[0] == "x":
+                tile_stats(source_tile(unit[1], half))
+
+        def norm(unit, half):
+            if unit[0] == "x":
+                tile_rstd(source_tile(unit[1], half))
+                tile_norm(source_tile(unit[1], half))
+
+        def turn(unit, half):
+            if unit[0] == "x":
+                turn_h(unit[1], half)
+            else:
+                turn_w(unit[1], half)
+
+        def quantise(unit):
+            if unit[0] == "x":
+                for g in range(PASSES):
+                    group_rows(unit[1], g)
+            for g in range(PASSES):
+                if unit[0] == "x":
+                    quantise_h(unit[1], g)
+                else:
+                    quantise_w(unit[1], g)
+
+        waiting = [(m, which) for which in range(OUT_COLS // CHANNELS) for m in range(X_TILES)]
+
+        def project_some(done, most):
+            able = [
+                (m, which)
+                for m, which in waiting
+                if ("x", m * P // QUARTER) in done and all(("w", PARTS * which + j) in done for j in range(PARTS))
+            ]
+            for m, which in able[:most]:
+                waiting.remove((m, which))
+                early = len(waiting) >= 16
+                last = len(waiting) < 2
+                project(m, which, 0 if last else 1 if early else m % 2, 2 if last else 1)
+
         with tc.manual_schedule():
-            tw(0, 0)
-            s1(0, 0)
-            s1(0, 1)
-            r1(0, 0)
-            r1(0, 1)
-            n1(0, 0)
-            n1(0, 1)
-            tw(0, 1)
-            s1(1, 0)
-            s1(1, 1)
-            tw(1, 0)
-            r1(1, 0)
-            r1(1, 1)
-            n1(1, 0)
-            n1(1, 1)
-            tx(0, 0)
-            tx(0, 1)
-            s1(2, 0)
-            s1(2, 1)
-            bs(0)
-            tw(1, 1)
-            r1(2, 0)
-            r1(2, 1)
-            n1(2, 0)
-            n1(2, 1)
-            tx(1, 0)
-            s1(3, 0)
-            s1(3, 1)
-            qw(0, 0)
-            qw(0, 1)
-            ih(0, 0)
-            ih(0, 1)
-            tw(2, 0)
-            r1(3, 0)
-            r1(3, 1)
-            n1(3, 0)
-            n1(3, 1)
-            qh(0, 0)
-            qh(0, 1)
-            tx(1, 1)
-            qw(1, 0)
-            qw(1, 1)
-            tw(2, 1)
-            pj(0, 0)
-            pj(1, 0)
-            ih(1, 0)
-            ih(1, 1)
-            qh(1, 0)
-            qh(1, 1)
-            tw(3, 0)
-            bs(1)
-            qw(2, 0)
-            qw(2, 1)
-            tx(2, 0)
-            tx(2, 1)
-            pj(2, 0)
-            pj(3, 0)
-            tw(3, 1)
-            bs(2)
-            qw(3, 0)
-            qw(3, 1)
-            pj(0, 1)
-            pj(1, 1)
-            ih(2, 0)
-            ih(2, 1)
-            qh(2, 0)
-            qh(2, 1)
-            tx(3, 0)
-            tx(3, 1)
-            pj(2, 1)
-            pj(3, 1)
-            tw(4, 0)
-            tw(4, 1)
-            pj(4, 0)
-            pj(5, 0)
-            ih(3, 0)
-            ih(3, 1)
-            qh(3, 0)
-            qh(3, 1)
-            qw(4, 0)
-            qw(4, 1)
-            pj(4, 1)
-            pj(5, 1)
-            tw(5, 0)
-            tw(5, 1)
-            pj(6, 0)
-            pj(7, 0)
-            qw(5, 0)
-            qw(5, 1)
-            pj(6, 1)
-            pj(7, 1)
-            pj(0, 2)
-            pj(1, 2)
-            pj(2, 2)
-            pj(3, 2)
-            pj(4, 2)
-            pj(5, 2)
-            pj(6, 2)
-            pj(7, 2)
+            for unit in units[:ahead]:
+                for half in range(2):
+                    statistics(unit, half)
+                    norm(unit, half)
+            for i in range(len(units) + projected):
+                for half in range(2):
+                    if i < len(units):
+                        turn(units[i], half)
+                    if half == 0 and i == 1:
+                        spread_bias()
+                    if i + ahead < len(units):
+                        statistics(units[i + ahead], half)
+                        norm(units[i + ahead], half)
+                    if half == 0 and 0 <= i - behind < len(units):
+                        quantise(units[i - behind])
+                if i >= projected:
+                    project_some(units[: i - projected + 1], 4)
+            project_some(units, len(waiting))

@@ -271,8 +271,8 @@ def tile_swintransformerblock_pa_kernel(
                 cols = slice(c * width, (c + 1) * width)
                 nc.sync.dma_start(out=out_rows[which][rows, cols], in_=result[:, cols])
 
-        units = [("w", 0), ("x", 0), ("w", 1), ("x", 1), ("w", 2), ("x", 2), ("w", 3), ("x", 3), ("w", 4), ("w", 5)]
-        ahead, behind, projected = 3, 2, 3
+        units = [("w", 0), ("x", 0), ("w", 1), ("x", 1), ("w", 2), ("w", 3), ("x", 2), ("w", 4), ("w", 5), ("x", 3)]
+        ahead, behind, projected = 3, 1, 2
 
         def statistics(unit, half):
             if unit[0] == "x":
@@ -309,9 +309,10 @@ def tile_swintransformerblock_pa_kernel(
             ]
             for m, which in able[:most]:
                 waiting.remove((m, which))
+                first = len(waiting) >= 22
                 early = len(waiting) >= 16
                 last = len(waiting) < 2
-                project(m, which, 0 if last else 1 if early else m % 2, 2 if last else 1)
+                project(m, which, 0 if first or last else 1 if early else m % 2, 2 if last else 1)
 
         with tc.manual_schedule():
             for unit in units[:ahead]:
@@ -322,7 +323,7 @@ def tile_swintransformerblock_pa_kernel(
                 for half in range(2):
                     if i < len(units):
                         turn(units[i], half)
-                    if half == 0 and i == 1:
+                    if half == 0 and i == 0:
                         spread_bias()
                     if i + ahead < len(units):
                         statistics(units[i + ahead], half)

from contextlib import ExitStack

import concourse.mybir as mybir
from concourse.masks import make_identity

F32 = mybir.dt.float32
BF16 = mybir.dt.bfloat16
U32 = mybir.dt.uint32
U8 = mybir.dt.uint8
I32 = mybir.dt.int32
FP8X4 = mybir.dt.float8_e4m3fn_x4
ALU = mybir.AluOpType
ACT = mybir.ActivationFunctionType

P = 128
TOKENS = 1024
CHANNELS = 1024
OUT_COLS = 3072
GRID = 32
SHIFT = 4
WINDOW = 8
WINDOWS_IN_ROW = GRID // WINDOW
GRID_ROWS_IN_TILE = P // GRID
EPS = 1e-5
Q_SCALE = 64 ** -0.5

PACK = 4
K_PASS = P * PACK
PASSES = CHANNELS // K_PASS
BANK = 512
W_BLOCKS = OUT_COLS // BANK
W_TILES = BANK // P
X_TILES = TOKENS // P
QUARTERS = 4
QUARTER_TILES = X_TILES // QUARTERS
QUARTER = QUARTER_TILES * P
PLANES = CHANNELS // P
BN_CHUNK = 512
PARTS = CHANNELS // BANK

FLOPS = 2 * TOKENS * CHANNELS * OUT_COLS


def tile_swintransformerblock_pa_kernel(
    tc, x, ln1_w, ln1_b, in_proj_w, in_proj_b, out_0, out_1, out_2
):
    nc = tc.nc
    x_rows = x.flatten_outer_dims()
    out_rows = [o.rearrange("w n h d -> (w n) (h d)") for o in (out_0, out_1, out_2)]

    with ExitStack() as stack:
        const = stack.enter_context(tc.tile_pool(name="const", bufs=1))
        keep = stack.enter_context(tc.tile_pool(name="keep", bufs=1))
        small = stack.enter_context(tc.tile_pool(name="small", bufs=X_TILES))
        normed = stack.enter_context(tc.tile_pool(name="normed", bufs=X_TILES))
        group_h = stack.enter_context(tc.tile_pool(name="group_h", bufs=4))
        group_w = stack.enter_context(tc.tile_pool(name="group_w", bufs=4))
        results = stack.enter_context(tc.tile_pool(name="results", bufs=8))
        psum = stack.enter_context(tc.psum_pool(name="psum", bufs=8))

        x_sb = [keep.tile([P, CHANNELS], BF16, name="x_sb%d" % s) for s in range(X_TILES)]
        w_raw = [keep.tile([P, W_TILES, CHANNELS], BF16, name="w_raw%d" % n) for n in range(W_BLOCKS)]

        def source_tile(q, i):
            return (q * QUARTER_TILES + i + 1) % X_TILES

        def load_x(q, i):
            s = source_tile(q, i)
            nc.sync.dma_start(out=x_sb[s][:], in_=x_rows[s * P : (s + 1) * P, :])

        def load_w(n, first, tiles):
            rows = in_proj_w[n * BANK + first * P : n * BANK + (first + tiles) * P, :]
            nc.sync.dma_start(
                out=w_raw[n][:, first : first + tiles, :], in_=rows.rearrange("(a p) k -> p a k", p=P)
            )

        bias_rows = const.tile([P, BANK], BF16)
        nc.vector.memset(bias_rows[:].bitcast(I32), 0)
        ln_gain_bf = const.tile([P, PASSES, PACK], BF16)
        ln_bias_bf = const.tile([P, PASSES, PACK], BF16)
        nc.scalar.dma_start(out=ln_gain_bf[:], in_=ln1_w.rearrange("(g p t) -> p g t", p=P, t=PACK))
        nc.scalar.dma_start(out=ln_bias_bf[:], in_=ln1_b.rearrange("(g p t) -> p g t", p=P, t=PACK))
        nc.scalar.dma_start(out=bias_rows[0:PARTS, :], in_=in_proj_b[0:CHANNELS].rearrange("(r c) -> r c", c=BANK))

        eps = const.tile([P, 1], F32)
        eps_rsqrt = const.tile([P, 1], F32)
        nc.vector.memset(eps[:], EPS)
        nc.scalar.activation(out=eps_rsqrt[:], in_=eps[:], func=ACT.Abs_reciprocal_sqrt)

        for i in range(QUARTER_TILES):
            load_x(0, i)
            load_w(0, i, 1)
        for i in range(QUARTER_TILES):
            load_x(1, i)
        load_w(0, W_TILES // 2, W_TILES // 2)
        for half in range(2):
            load_w(1, half * W_TILES // 2, W_TILES // 2)
            load_x(2, half)
        for n in range(2, W_BLOCKS):
            for half in range(2):
                load_w(n, half * W_TILES // 2, W_TILES // 2)
            if n == 2:
                for i in range(QUARTER_TILES):
                    load_x(3, i)
        bias = const.tile([P, OUT_COLS], BF16)
        for which in range(1, OUT_COLS // CHANNELS):
            cols = slice(which * CHANNELS, (which + 1) * CHANNELS)
            nc.sync.dma_start(out=bias[:, cols], in_=in_proj_b[cols].partition_broadcast(P))

        ident = const.tile([P, P], F32)
        make_identity(nc, ident[:])
        ident_rows = ident[:].rearrange("p (i j) -> p i j", j=GRID)
        rotated = const.tile([P, GRID_ROWS_IN_TILE, GRID], F32)
        nc.gpsimd.tensor_copy(out=rotated[:, :, 0 : GRID - SHIFT], in_=ident_rows[:, :, SHIFT:GRID])
        nc.gpsimd.tensor_copy(out=rotated[:, :, GRID - SHIFT : GRID], in_=ident_rows[:, :, 0:SHIFT])
        perm = const.tile([P, WINDOWS_IN_ROW, GRID_ROWS_IN_TILE, WINDOW], F32)
        nc.gpsimd.tensor_copy(out=perm[:], in_=rotated[:].rearrange("p i (w c) -> p w i c", c=WINDOW))
        perm_2d = perm[:].rearrange("p w i c -> p (w i c)")
        pick = const.tile([P, PARTS], BF16)
        nc.gpsimd.tensor_scalar(
            out=pick[:], in0=ident[:, 0:PARTS], scalar1=Q_SCALE, scalar2=0.0, op0=ALU.mult, op1=ALU.add
        )
        ln_gain = const.tile([P, PASSES, PACK], F32)
        ln_bias = const.tile([P, PASSES, PACK], F32)
        nc.gpsimd.tensor_copy(out=ln_gain[:], in_=ln_gain_bf[:])
        nc.gpsimd.tensor_copy(out=ln_bias[:], in_=ln_bias_bf[:])

        def spread_bias():
            spread = psum.tile([P, CHANNELS], BF16, tag="bank")
            for r in range(PARTS):
                nc.tensor.matmul(
                    out=spread[:, r * BANK : (r + 1) * BANK],
                    lhsT=pick[:, r : r + 1].to_broadcast([P, P]),
                    rhs=bias_rows[:],
                    start=True,
                    stop=True,
                )
            nc.scalar.copy(out=bias[:, 0:CHANNELS], in_=spread[:])

        def out_scale(n):
            return Q_SCALE if n * BANK < CHANNELS else 1.0

        h_codes = keep.tile([P, PASSES, TOKENS], U32, align_bytes=64)
        h_scales = keep.tile([P, PASSES, TOKENS], U8, align_bytes=64)
        w_codes = keep.tile([P, W_BLOCKS, PASSES, BANK], U32, align_bytes=64)
        w_scales = keep.tile([P, W_BLOCKS, PASSES, BANK], U8, align_bytes=64)
        planes = [keep.tile([P, PLANES, QUARTER], BF16, name="planes%d" % q) for q in range(QUARTERS)]
        mean_var = {}
        neg_mean = {}
        rstd = {}
        xn = {}
        grouped_h = {}
        grouped_w = {}

        def tile_stats(s):
            stats = small.tile([P, CHANNELS // BN_CHUNK, 6], F32, tag="stats")
            for c in range(CHANNELS // BN_CHUNK):
                nc.vector.bn_stats(out=stats[:, c, :], in_=x_sb[s][:, c * BN_CHUNK : (c + 1) * BN_CHUNK])
            mean_var[s] = small.tile([P, 2], F32, name="mean_var", tag="mean_var")
            nc.vector.bn_aggr(out=mean_var[s][:], in_=stats[:].rearrange("p c s -> p (c s)"))

        def tile_rstd(s):
            neg_mean[s] = small.tile([P, 1], F32, name="neg_mean", tag="neg_mean")
            nc.gpsimd.tensor_scalar(
                out=neg_mean[s][:], in0=mean_var[s][:, 0:1], scalar1=-1.0, scalar2=0.0, op0=ALU.mult, op1=ALU.add
            )
            rstd[s] = small.tile([P, 1], F32, name="rstd", tag="rstd")
            nc.scalar.activation(
                out=rstd[s][:], in_=mean_var[s][:, 1:2], func=ACT.Abs_reciprocal_sqrt, bias=eps[:, 0:1]
            )

        def tile_norm(s):
            xn[s] = normed.tile([P, PACK, CHANNELS // PACK], F32, name="xn", tag="xn")
            nc.gpsimd.tensor_scalar(
                out=xn[s][:],
                in0=x_sb[s][:].rearrange("p (w t) -> p t w", t=PACK),
                scalar1=neg_mean[s][:, 0:1],
                scalar2=rstd[s][:, 0:1],
                op0=ALU.add,
                op1=ALU.mult,
            )

        def turn_h(q, g):
            for t0 in range(0, PACK, 2):
                turned = psum.tile([P, 2, WINDOWS_IN_ROW, QUARTER_TILES, P // WINDOWS_IN_ROW], F32, tag="bank")
                for t in (t0, t0 + 1):
                    for hb in range(QUARTER_TILES):
                        nc.tensor.transpose(
                            out=turned[:, t - t0, :, hb, :],
                            in_=xn[source_tile(q, hb)][:, t, g * P : (g + 1) * P],
                            identity=perm_2d,
                        )
                for t in (t0, t0 + 1):
                    nc.scalar.activation(
                        out=planes[q][:, PACK * g + t, :],
                        in_=turned[:, t - t0, :, :, :].rearrange("p w b c -> p (w b c)"),
                        func=ACT.Identity,
                        scale=ln_gain[:, g, t : t + 1],
                        bias=ln_bias[:, g, t : t + 1],
                    )

        def group_rows(q, g):
            grouped_h[q, g] = group_h.tile([P, QUARTER, PACK], BF16, align_bytes=64, name="grouped_h", tag="grouped_h")
            nc.vector.tensor_copy(
                out=grouped_h[q, g][:].rearrange("p (c i) t -> p c t i", i=4),
                in_=planes[q][:, PACK * g : PACK * (g + 1), :].rearrange("p t (c i) -> p c t i", i=4),
            )

        def quantise_h(q, g):
            rows = slice(q * QUARTER, (q + 1) * QUARTER)
            nc.vector.quantize_mx(
                out=h_codes[:, g, rows].bitcast(FP8X4),
                scales=h_scales[:, g, rows],
                in_=grouped_h[q, g][:].rearrange("p c t -> p (c t)"),
            )

        def turn_w(n, pair):
            words = w_raw[n][:].bitcast(F32)
            for g in range(PASSES):
                if pair == 0:
                    grouped_w[n, g] = group_w.tile([P, BANK, PACK], BF16, align_bytes=64, name="grouped_w", tag="grouped_w")
                turned = psum.tile([P, 2, 2, P], F32, tag="bank")
                for u in range(2):
                    for a2 in range(2):
                        first = 2 * g * P + u
                        nc.tensor.transpose(
                            out=turned[:, u, a2, :],
                            in_=words[:, 2 * pair + a2, first : 2 * (g + 1) * P : 2],
                            identity=ident[:],
                        )
                nc.scalar.copy(
                    out=grouped_w[n, g][:].bitcast(F32)[:, 2 * pair * P : 2 * (pair + 1) * P, :],
                    in_=turned[:].rearrange("p u a c -> p (a c) u"),
                )

        def quantise_w(n, g):
            nc.vector.quantize_mx(
                out=w_codes[:, n, g, :].bitcast(FP8X4),
                scales=w_scales[:, n, g, :],
                in_=grouped_w[n, g][:].rearrange("p c t -> p (c t)"),
            )

        def project(m, which, banks_of_scalar, stores):
            rows = slice(m * P, (m + 1) * P)
            blocks = range(PARTS * which, PARTS * (which + 1))
            accs = [psum.tile([P, BANK], F32, name="acc", tag="bank") for n in blocks]
            for acc, n in zip(accs, blocks):
                for g in range(PASSES):
                    nc.tensor.matmul_mx(
                        out=acc[:],
                        lhsT=h_codes[:, g, rows].bitcast(FP8X4),
                        lhsT_scale=h_scales[:, g, rows],
                        rhs=w_codes[:, n, g, :].bitcast(FP8X4),
                        rhs_scale=w_scales[:, n, g, :],
                        start=(g == 0),
                        stop=(g == PASSES - 1),
                    )
            result = results.tile([P, CHANNELS], F32, name="result", tag="result")
            for j, (acc, n) in enumerate(zip(accs, blocks)):
                piece = result[:, j * BANK : (j + 1) * BANK]
                cols = slice(n * BANK, (n + 1) * BANK)
                if j < banks_of_scalar:
                    nc.scalar.mul(out=piece, in_=acc[:], mul=out_scale(n))
                    nc.gpsimd.tensor_tensor(out=piece, in0=piece, in1=bias[:, cols], op=ALU.add)
                else:
                    nc.vector.scalar_tensor_tensor(
                        out=piece, in0=acc[:], scalar=out_scale(n), in1=bias[:, cols], op0=ALU.mult, op1=ALU.add
                    )
            width = CHANNELS // stores
            for c in range(stores):
                cols = slice(c * width, (c + 1) * width)
                nc.sync.dma_start(out=out_rows[which][rows, cols], in_=result[:, cols])

        units = [("w", 0), ("x", 0), ("w", 1), ("x", 1), ("w", 2), ("w", 3), ("x", 2), ("w", 4), ("w", 5), ("x", 3)]
        ahead, behind, projected = 3, 1, 2

        def statistics(unit, half):
            if unit[0] == "x":
                tile_stats(source_tile(unit[1], half))

        def norm(unit, half):
            if unit[0] == "x":
                tile_rstd(source_tile(unit[1], half))
                tile_norm(source_tile(unit[1], half))

        def turn(unit, half):
            if unit[0] == "x":
                turn_h(unit[1], half)
            else:
                turn_w(unit[1], half)

        def quantise(unit):
            if unit[0] == "x":
                for g in range(PASSES):
                    group_rows(unit[1], g)
            for g in range(PASSES):
                if unit[0] == "x":
                    quantise_h(unit[1], g)
                else:
                    quantise_w(unit[1], g)

        waiting = [(m, which) for which in range(OUT_COLS // CHANNELS) for m in range(X_TILES)]

        def project_some(done, most):
            able = [
                (m, which)
                for m, which in waiting
                if ("x", m * P // QUARTER) in done and all(("w", PARTS * which + j) in done for j in range(PARTS))
            ]
            for m, which in able[:most]:
                waiting.remove((m, which))
                first = len(waiting) >= 22
                early = len(waiting) >= 16
                last = len(waiting) < 2
                project(m, which, 0 if first or last else 1 if early else m % 2, 2 if last else 1)

        with tc.manual_schedule():
            for unit in units[:ahead]:
                for half in range(2):
                    statistics(unit, half)
                    norm(unit, half)
            for i in range(len(units) + projected):
                for half in range(2):
                    if i < len(units):
                        turn(units[i], half)
                    if half == 0 and i == 0:
                        spread_bias()
                    if i + ahead < len(units):
                        statistics(units[i + ahead], half)
                        norm(units[i + ahead], half)
                    if half == 0 and 0 <= i - behind < len(units):
                        quantise(units[i - behind])
                if i >= projected:
                    project_some(units[: i - projected + 1], 4)
            project_some(units, len(waiting))
